import numpy as np
import ml_dtypes


def mxq(x, axis, fmt="e4m3"):
    dtype, down = {"e4m3": (ml_dtypes.float8_e4m3fn, 7), "e5m2": (ml_dtypes.float8_e5m2, 14)}[fmt]
    v = np.moveaxis(np.asarray(x, np.float32).astype(ml_dtypes.bfloat16).astype(np.float64), axis, -1)
    blocks = v.reshape(v.shape[:-1] + (-1, 32))
    amax = np.abs(blocks).max(-1, keepdims=True)
    byte = np.maximum(np.where(amax > 0, np.frexp(amax)[1] - 1 + 127, 0) - down, 1)
    scale = np.exp2(byte - 127.0)
    codes = (blocks / scale).astype(np.float32).astype(dtype).astype(np.float64)
    return np.moveaxis((codes * scale).reshape(v.shape), -1, axis)


WIDE = False


def mx_kscale(k):
    if not WIDE:
        return np.ones(k)
    levels = np.array([10, -10, 5, -5, 0])
    a = np.random.permutation(np.resize(levels, k // 512 * 4)).reshape(k // 512, 4)
    idx = np.arange(k)
    return np.exp2(a[idx // 512, idx % 128 // 32])


BF16 = ml_dtypes.bfloat16


def bf(x):
    return np.asarray(x, np.float32).astype(BF16)


def f64(x):
    return np.asarray(x).astype(np.float64)


B, S, K, C_IN, H, HO = 8, 112, 16, 768, 2048, 2048
N = S + K
BN_EPS = 1e-5


def group_bn(z, g, b):
    m = z.mean(axis=1, keepdims=True)
    v = z.var(axis=1, keepdims=True)
    return (z - m) * (1.0 / np.sqrt(v + BN_EPS)) * g + b


def setup_inputs():
    t = mx_kscale(H)
    sd = 2.0 * np.exp2(-12.0 * np.random.random((B, 1, H)))
    z1 = sd * (np.random.standard_normal((B, N, H)) + 0.5 * np.random.standard_normal((B, 1, H)))
    return {"z1": bf(z1),
            "g1": bf((1.0 + 0.3 * np.random.standard_normal(H)) * t),
            "be1": bf(0.3 * np.random.standard_normal(H) * t),
            "W2": bf(np.random.standard_normal((H, HO)) / np.sqrt(H) / t[:, None]),
            "b2": bf(np.random.standard_normal(HO))}


def reference(z1, g1, be1, W2, b2):
    h = np.maximum(group_bn(f64(z1), f64(g1), f64(be1)), 0.0)
    return (mxq(h, 2, "e4m3") @ mxq(f64(W2), 0, "e4m3")) + f64(b2)

@@ -1,0 +1,268 @@
+from contextlib import ExitStack
+
+import concourse.mybir as mybir
+from concourse.masks import make_identity
+
+FP8X4 = mybir.dt.float8_e4m3fn_x4
+BF16 = mybir.dt.bfloat16
+F32 = mybir.dt.float32
+U32 = mybir.dt.uint32
+U8 = mybir.dt.uint8
+ACT = mybir.ActivationFunctionType
+ALU = mybir.AluOpType
+
+P = 128
+PACK = 4
+GROUPS = 8
+H = 2048
+HO = 2048
+K_PASSES = H // (P * PACK)
+CHUNKS = H // P
+N_TILE = 512
+N_BLOCKS = HO // N_TILE
+BN_EPS = 1e-5
+
+PAIRS = 2 * GROUPS
+PAIR_CHUNKS = 2 * PACK
+W_OPERANDS = N_BLOCKS * K_PASSES
+W_AHEAD = 2
+ACC_BANKS = 4
+
+FLOPS = 2 * GROUPS * P * H * HO
+
+
+def interleave(nc, grouped, planes):
+    nc.vector.tensor_copy(
+        out=grouped.rearrange("p (m i) t -> p m t i", i=4),
+        in_=planes.rearrange("p t (m i) -> p m t i", i=4),
+    )
+
+
+def tile_vocohead_pa_kernel(tc, z1, g1, be1, W2, b2, out):
+    nc = tc.nc
+    with ExitStack() as ctx:
+        const = ctx.enter_context(tc.tile_pool(name="const", bufs=1))
+        inputs = ctx.enter_context(tc.tile_pool(name="inputs", bufs=1))
+        keep = ctx.enter_context(tc.tile_pool(name="keep", bufs=1))
+        stage = ctx.enter_context(tc.tile_pool(name="stage", bufs=3))
+        stats = ctx.enter_context(tc.tile_pool(name="stats", bufs=4))
+        results = ctx.enter_context(tc.tile_pool(name="results", bufs=6))
+        centred_pool = ctx.enter_context(tc.psum_pool(name="centred", bufs=4))
+        acc_pool = ctx.enter_context(tc.psum_pool(name="acc", bufs=ACC_BANKS))
+
+        gb_rows = const.tile([P, P], BF16)
+        nc.vector.memset(gb_rows[32:64, :], 0.0)
+        nc.vector.memset(gb_rows[64:128, :], 0.0)
+        nc.scalar.dma_start(out=gb_rows[0:CHUNKS, :], in_=g1.rearrange("(a p) -> a p", p=P))
+        nc.scalar.dma_start(
+            out=gb_rows[CHUNKS : 2 * CHUNKS, :], in_=be1.rearrange("(a p) -> a p", p=P)
+        )
+        b2_all = const.tile([P, HO], BF16)
+        z_sb = []
+        w_raw = []
+
+        def load_weights(k):
+            nb, c = divmod(k, K_PASSES)
+            w_tile = inputs.tile([P, PACK, N_TILE], BF16, name="w%d" % k)
+            nc.sync.dma_start(
+                out=w_tile[:],
+                in_=W2[
+                    c * PACK * P : (c + 1) * PACK * P, nb * N_TILE : (nb + 1) * N_TILE
+                ].rearrange("(t p) n -> p t n", p=P),
+            )
+            w_raw.append(w_tile)
+
+        for b in range(GROUPS):
+            load_weights(2 * b)
+            z_tile = inputs.tile([P, H], BF16, name="z%d" % b)
+            nc.sync.dma_start(out=z_tile[:], in_=z1[b])
+            z_sb.append(z_tile)
+            load_weights(2 * b + 1)
+            if b == 1:
+                nc.sync.dma_start(out=b2_all[:], in_=b2.partition_broadcast(P))
+
+        ident = const.tile([P, P], BF16)
+        make_identity(nc, ident[:])
+        centre_matrix = const.tile([P, P], BF16)
+        nc.vector.tensor_scalar_add(out=centre_matrix[:], in0=ident[:], scalar1=-1.0 / P)
+        one = const.tile([P, 1], F32)
+        nc.vector.memset(one[:], 1.0)
+        warm = const.tile([P, 1], F32)
+        nc.scalar.activation(out=warm[:], in_=one[:], func=ACT.Sqrt)
+
+        gb_ps = centred_pool.tile([P, P], BF16, tag="centred")
+        nc.tensor.transpose(out=gb_ps[:], in_=gb_rows[:], identity=ident[:])
+        gain0 = const.tile([P, CHUNKS], F32)
+        nc.vector.tensor_scalar_mul(out=gain0[:], in0=gb_ps[:, 0:CHUNKS], scalar1=BN_EPS**-0.5)
+        shift = const.tile([P, CHUNKS], F32)
+        nc.vector.tensor_copy(out=shift[:], in_=gb_ps[:, CHUNKS : 2 * CHUNKS])
+
+        w_codes = keep.tile([P, W_OPERANDS, N_TILE], U32, align_bytes=64)
+        w_scales = keep.tile([P, W_OPERANDS, N_TILE], U8, align_bytes=64)
+        h_codes = keep.tile([P, PAIRS, 2 * P], U32, align_bytes=64)
+        h_scales = keep.tile([P, PAIRS, 2 * P], U8, align_bytes=64)
+
+        banks = {}
+        sumsq = {}
+        spread = {}
+        inverse = {}
+        gain = {}
+        planes = {}
+        h_grouped = {}
+        w_grouped = {}
+
+        def centre(pair, j):
+            b, first = pair // 2, (pair % 2) * PAIR_CHUNKS + j * PACK
+            bank = centred_pool.tile([P, PACK, P], F32, tag="centred")
+            for t in range(PACK):
+                a = first + t
+                nc.tensor.matmul(
+                    out=bank[:, t, :],
+                    lhsT=z_sb[b][:, a * P : (a + 1) * P],
+                    rhs=centre_matrix[:],
+                    start=True,
+                    stop=True,
+                )
+            banks[(pair, j)] = bank
+
+        def squares(pair):
+            sumsq[pair] = stats.tile([P, PAIR_CHUNKS], F32, name="sumsq")
+            unread = stage.tile([P, PAIR_CHUNKS, P], BF16, name="unread")
+            for i in range(PAIR_CHUNKS):
+                nc.scalar.activation(
+                    out=unread[:, i, :],
+                    in_=banks[(pair, i // PACK)][:, i % PACK, :],
+                    func=ACT.Square,
+                    accum_out=sumsq[pair][:, i : i + 1],
+                )
+
+        def root(pair):
+            spread[pair] = stats.tile([P, PAIR_CHUNKS], F32, name="spread")
+            nc.scalar.activation(
+                out=spread[pair][:],
+                in_=sumsq[pair][:],
+                func=ACT.Sqrt,
+                bias=one[:, 0:1],
+                scale=1.0 / (P * BN_EPS),
+            )
+
+        def invert(pair):
+            inverse[pair] = stats.tile([P, PAIR_CHUNKS], F32, name="inverse")
+            nc.vector.reciprocal(out=inverse[pair][:], in_=spread[pair][:])
+
+        def scale_gain(pair):
+            first = (pair % 2) * PAIR_CHUNKS
+            gain[pair] = stats.tile([P, PAIR_CHUNKS], F32, name="gain")
+            nc.vector.tensor_mul(
+                out=gain[pair][:], in0=inverse[pair][:], in1=gain0[:, first : first + PAIR_CHUNKS]
+            )
+
+        def normalise(pair, j):
+            if j == 0:
+                planes[pair] = stage.tile([P, PACK, 2, P], BF16, name="planes")
+            for t in range(PACK):
+                i = j * PACK + t
+                a = (pair % 2) * PAIR_CHUNKS + i
+                nc.scalar.activation(
+                    out=planes[pair][:, t, j, :],
+                    in_=banks[(pair, j)][:, t, :],
+                    func=ACT.Relu,
+                    bias=shift[:, a : a + 1],
+                    scale=gain[pair][:, i : i + 1],
+                )
+
+        def interleave_h(pair):
+            h_grouped[pair] = stage.tile([P, 2 * P, PACK], BF16, align_bytes=64, name="h_grouped")
+            interleave(nc, h_grouped[pair][:], planes[pair][:].rearrange("p t j r -> p t (j r)"))
+
+        def quantise_h(pair):
+            nc.vector.quantize_mx(
+                out=h_codes[:, pair, :].bitcast(FP8X4),
+                scales=h_scales[:, pair, :],
+                in_=h_grouped[pair][:].rearrange("p n t -> p (n t)"),
+            )
+
+        def interleave_w(k):
+            w_grouped[k] = stage.tile([P, N_TILE, PACK], BF16, align_bytes=64, name="w_grouped")
+            interleave(nc, w_grouped[k][:], w_raw[k][:])
+
+        def quantise_w(k):
+            nc.vector.quantize_mx(
+                out=w_codes[:, k, :].bitcast(FP8X4),
+                scales=w_scales[:, k, :],
+                in_=w_grouped[k][:].rearrange("p n t -> p (n t)"),
+            )
+
+        def multiply(b, nb):
+            acc = acc_pool.tile([P, N_TILE], F32, name="acc")
+            for c in range(K_PASSES):
+                rows = slice((c % 2) * P, (c % 2 + 1) * P)
+                nc.tensor.matmul_mx(
+                    out=acc[:],
+                    lhsT=h_codes[:, 2 * b + c // 2, rows].bitcast(FP8X4),
+                    lhsT_scale=h_scales[:, 2 * b + c // 2, rows],
+                    rhs=w_codes[:, K_PASSES * nb + c, :].bitcast(FP8X4),
+                    rhs_scale=w_scales[:, K_PASSES * nb + c, :],
+                    start=(c == 0),
+                    stop=(c == K_PASSES - 1),
+                )
+            return acc
+
+        def add_bias_and_store(acc, b, nb):
+            cols = slice(nb * N_TILE, (nb + 1) * N_TILE)
+            result = results.tile([P, N_TILE], F32, name="result")
+            nc.vector.tensor_tensor(out=result[:], in0=acc[:], in1=b2_all[:, cols], op=ALU.add)
+            nc.sync.dma_start(out=out[b, :, cols], in_=result[:])
+
+        with tc.manual_schedule():
+            for pair in (0, 1):
+                centre(pair, 0)
+                centre(pair, 1)
+            for k in range(W_AHEAD):
+                interleave_w(k)
+            for k in range(W_AHEAD):
+                quantise_w(k)
+            squares(0)
+            root(0)
+            invert(0)
+            scale_gain(0)
+
+            multiplied = set()
+            in_psum = []
+            slot = 0
+            while len(multiplied) < GROUPS * N_BLOCKS or in_psum:
+                if slot + 1 < PAIRS:
+                    squares(slot + 1)
+                for j in range(2):
+                    if slot < PAIRS:
+                        normalise(slot, j)
+                    if slot + 2 < PAIRS:
+                        centre(slot + 2, j)
+                    if j == 0 and slot + 1 < PAIRS:
+                        root(slot + 1)
+
+                k = slot + W_AHEAD
+                if slot + 1 < PAIRS:
+                    invert(slot + 1)
+                if 1 <= slot <= PAIRS:
+                    interleave_h(slot - 1)
+                if slot + 1 < PAIRS:
+                    scale_gain(slot + 1)
+                if k < W_OPERANDS:
+                    interleave_w(k)
+                if 1 <= slot <= PAIRS:
+                    quantise_h(slot - 1)
+                for acc, b, nb in in_psum:
+                    add_bias_and_store(acc, b, nb)
+                in_psum = []
+                if k < W_OPERANDS:
+                    quantise_w(k)
+
+                groups_ready = min(slot // 2, GROUPS)
+                blocks_ready = min(k + 1, W_OPERANDS) // K_PASSES
+                for b in range(groups_ready):
+                    for nb in range(blocks_ready):
+                        if (b, nb) not in multiplied and len(in_psum) < ACC_BANKS:
+                            multiplied.add((b, nb))
+                            in_psum.append((multiply(b, nb), b, nb))
+                slot += 1

@@ -214,55 +214,54 @@ def tile_vocohead_pa_kernel(tc, z1, g1, be1, W2, b2, out):
             nc.vector.tensor_tensor(out=result[:], in0=acc[:], in1=b2_all[:, cols], op=ALU.add)
             nc.sync.dma_start(out=out[b, :, cols], in_=result[:])
 
-        with tc.manual_schedule():
-            for pair in (0, 1):
-                centre(pair, 0)
-                centre(pair, 1)
-            for k in range(W_AHEAD):
+        for pair in (0, 1):
+            centre(pair, 0)
+            centre(pair, 1)
+        for k in range(W_AHEAD):
+            interleave_w(k)
+        for k in range(W_AHEAD):
+            quantise_w(k)
+        squares(0)
+        root(0)
+        invert(0)
+        scale_gain(0)
+
+        multiplied = set()
+        in_psum = []
+        slot = 0
+        while len(multiplied) < GROUPS * N_BLOCKS or in_psum:
+            if slot + 1 < PAIRS:
+                squares(slot + 1)
+            for j in range(2):
+                if slot < PAIRS:
+                    normalise(slot, j)
+                if slot + 2 < PAIRS:
+                    centre(slot + 2, j)
+                if j == 0 and slot + 1 < PAIRS:
+                    root(slot + 1)
+
+            k = slot + W_AHEAD
+            if slot + 1 < PAIRS:
+                invert(slot + 1)
+            if 1 <= slot <= PAIRS:
+                interleave_h(slot - 1)
+            if slot + 1 < PAIRS:
+                scale_gain(slot + 1)
+            if k < W_OPERANDS:
                 interleave_w(k)
-            for k in range(W_AHEAD):
-                quantise_w(k)
-            squares(0)
-            root(0)
-            invert(0)
-            scale_gain(0)
-
-            multiplied = set()
+            if 1 <= slot <= PAIRS:
+                quantise_h(slot - 1)
+            for acc, b, nb in in_psum:
+                add_bias_and_store(acc, b, nb)
             in_psum = []
-            slot = 0
-            while len(multiplied) < GROUPS * N_BLOCKS or in_psum:
-                if slot + 1 < PAIRS:
-                    squares(slot + 1)
-                for j in range(2):
-                    if slot < PAIRS:
-                        normalise(slot, j)
-                    if slot + 2 < PAIRS:
-                        centre(slot + 2, j)
-                    if j == 0 and slot + 1 < PAIRS:
-                        root(slot + 1)
+            if k < W_OPERANDS:
+                quantise_w(k)
 
-                k = slot + W_AHEAD
-                if slot + 1 < PAIRS:
-                    invert(slot + 1)
-                if 1 <= slot <= PAIRS:
-                    interleave_h(slot - 1)
-                if slot + 1 < PAIRS:
-                    scale_gain(slot + 1)
-                if k < W_OPERANDS:
-                    interleave_w(k)
-                if 1 <= slot <= PAIRS:
-                    quantise_h(slot - 1)
-                for acc, b, nb in in_psum:
-                    add_bias_and_store(acc, b, nb)
-                in_psum = []
-                if k < W_OPERANDS:
-                    quantise_w(k)
-
-                groups_ready = min(slot // 2, GROUPS)
-                blocks_ready = min(k + 1, W_OPERANDS) // K_PASSES
-                for b in range(groups_ready):
-                    for nb in range(blocks_ready):
-                        if (b, nb) not in multiplied and len(in_psum) < ACC_BANKS:
-                            multiplied.add((b, nb))
-                            in_psum.append((multiply(b, nb), b, nb))
-                slot += 1
+            groups_ready = min(slot // 2, GROUPS)
+            blocks_ready = min(k + 1, W_OPERANDS) // K_PASSES
+            for b in range(groups_ready):
+                for nb in range(blocks_ready):
+                    if (b, nb) not in multiplied and len(in_psum) < ACC_BANKS:
+                        multiplied.add((b, nb))
+                        in_psum.append((multiply(b, nb), b, nb))
+            slot += 1

@@ -50,14 +50,13 @@ def tile_vocohead_pa_kernel(tc, z1, g1, be1, W2, b2, out):
         centred_pool = ctx.enter_context(tc.psum_pool(name="centred", bufs=4))
         acc_pool = ctx.enter_context(tc.psum_pool(name="acc", bufs=ACC_BANKS))
 
-        gb_rows = const.tile([P, P], BF16)
-        nc.vector.memset(gb_rows[32:64, :], 0.0)
-        nc.vector.memset(gb_rows[64:128, :], 0.0)
-        nc.scalar.dma_start(out=gb_rows[0:CHUNKS, :], in_=g1.rearrange("(a p) -> a p", p=P))
-        nc.scalar.dma_start(
-            out=gb_rows[CHUNKS : 2 * CHUNKS, :], in_=be1.rearrange("(a p) -> a p", p=P)
-        )
-        b2_all = const.tile([P, HO], BF16)
+        vector_rows = const.tile([P, P], BF16)
+        nc.vector.memset(vector_rows[64:128, :], 0.0)
+        for i, vector in enumerate((g1, be1, b2, b2)):
+            nc.scalar.dma_start(
+                out=vector_rows[i * CHUNKS : (i + 1) * CHUNKS, :],
+                in_=vector.rearrange("(a p) -> a p", p=P),
+            )
         z_sb = []
         w_raw = []
 
@@ -78,8 +77,6 @@ def tile_vocohead_pa_kernel(tc, z1, g1, be1, W2, b2, out):
             nc.sync.dma_start(out=z_tile[:], in_=z1[b])
             z_sb.append(z_tile)
             load_weights(2 * b + 1)
-            if b == 1:
-                nc.sync.dma_start(out=b2_all[:], in_=b2.partition_broadcast(P))
 
         ident = const.tile([P, P], BF16)
         make_identity(nc, ident[:])
@@ -90,12 +87,14 @@ def tile_vocohead_pa_kernel(tc, z1, g1, be1, W2, b2, out):
         warm = const.tile([P, 1], F32)
         nc.scalar.activation(out=warm[:], in_=one[:], func=ACT.Sqrt)
 
-        gb_ps = centred_pool.tile([P, P], BF16, tag="centred")
-        nc.tensor.transpose(out=gb_ps[:], in_=gb_rows[:], identity=ident[:])
+        columns_ps = centred_pool.tile([P, P], BF16, tag="centred")
+        nc.tensor.transpose(out=columns_ps[:], in_=vector_rows[:], identity=ident[:])
         gain0 = const.tile([P, CHUNKS], F32)
-        nc.vector.tensor_scalar_mul(out=gain0[:], in0=gb_ps[:, 0:CHUNKS], scalar1=BN_EPS**-0.5)
+        nc.vector.tensor_scalar_mul(out=gain0[:], in0=columns_ps[:, 0:CHUNKS], scalar1=BN_EPS**-0.5)
         shift = const.tile([P, CHUNKS], F32)
-        nc.vector.tensor_copy(out=shift[:], in_=gb_ps[:, CHUNKS : 2 * CHUNKS])
+        nc.vector.tensor_copy(out=shift[:], in_=columns_ps[:, CHUNKS : 2 * CHUNKS])
+        b2_columns = const.tile([P, CHUNKS], BF16)
+        nc.vector.tensor_copy(out=b2_columns[:], in_=columns_ps[:, 2 * CHUNKS : 3 * CHUNKS])
 
         w_codes = keep.tile([P, W_OPERANDS, N_TILE], U32, align_bytes=64)
         w_scales = keep.tile([P, W_OPERANDS, N_TILE], U8, align_bytes=64)
@@ -172,14 +171,18 @@ def tile_vocohead_pa_kernel(tc, z1, g1, be1, W2, b2, out):
                 )
 
         def interleave_h(pair):
-            h_grouped[pair] = stage.tile([P, 2 * P, PACK], BF16, align_bytes=64, name="h_grouped")
-            interleave(nc, h_grouped[pair][:], planes[pair][:].rearrange("p t j r -> p t (j r)"))
+            h_grouped[pair] = stage.tile([P, 2, P, PACK], BF16, align_bytes=64, name="h_grouped")
+            nc.scalar.copy(
+                out=h_grouped[pair][:, 0, :, :].rearrange("p (m i) t -> p m t i", i=4),
+                in_=planes[pair][:, :, 0, :].rearrange("p t (m i) -> p m t i", i=4),
+            )
+            interleave(nc, h_grouped[pair][:, 1, :, :], planes[pair][:, :, 1, :])
 
         def quantise_h(pair):
             nc.vector.quantize_mx(
                 out=h_codes[:, pair, :].bitcast(FP8X4),
                 scales=h_scales[:, pair, :],
-                in_=h_grouped[pair][:].rearrange("p n t -> p (n t)"),
+                in_=h_grouped[pair][:].rearrange("p j r t -> p (j r t)"),
             )
 
         def interleave_w(k):
@@ -225,6 +228,23 @@ def tile_vocohead_pa_kernel(tc, z1, g1, be1, W2, b2, out):
         root(0)
         invert(0)
         scale_gain(0)
+
+        b2_all = const.tile([P, HO], BF16)
+        for nb in range(N_BLOCKS):
+            b2_ps = acc_pool.tile([P, PACK, P], F32, name="acc")
+            for t in range(PACK):
+                a = PACK * nb + t
+                nc.tensor.matmul(
+                    out=b2_ps[:, t, :],
+                    lhsT=b2_columns[:, a : a + 1].to_broadcast([P, P]),
+                    rhs=ident[:],
+                    start=True,
+                    stop=True,
+                )
+            nc.vector.tensor_copy(
+                out=b2_all[:, nb * N_TILE : (nb + 1) * N_TILE],
+                in_=b2_ps[:].rearrange("p t n -> p (t n)"),
+            )
 
         multiplied = set()
         in_psum = []

@@ -71,12 +71,12 @@ def tile_vocohead_pa_kernel(tc, z1, g1, be1, W2, b2, out):
             )
             w_raw.append(w_tile)
 
-        for b in range(GROUPS):
-            load_weights(2 * b)
-            z_tile = inputs.tile([P, H], BF16, name="z%d" % b)
-            nc.sync.dma_start(out=z_tile[:], in_=z1[b])
+        for pair in range(PAIRS):
+            half = slice((pair % 2) * (H // 2), (pair % 2 + 1) * (H // 2))
+            z_tile = inputs.tile([P, H // 2], BF16, name="z%d" % pair)
+            nc.sync.dma_start(out=z_tile[:], in_=z1[pair // 2, :, half])
             z_sb.append(z_tile)
-            load_weights(2 * b + 1)
+            load_weights(pair)
 
         ident = const.tile([P, P], BF16)
         make_identity(nc, ident[:])
@@ -85,7 +85,7 @@ def tile_vocohead_pa_kernel(tc, z1, g1, be1, W2, b2, out):
         one = const.tile([P, 1], F32)
         nc.vector.memset(one[:], 1.0)
         warm = const.tile([P, 1], F32)
-        nc.scalar.activation(out=warm[:], in_=one[:], func=ACT.Sqrt)
+        nc.scalar.activation(out=warm[:], in_=one[:], func=ACT.Abs_reciprocal_sqrt)
 
         columns_ps = centred_pool.tile([P, P], BF16, tag="centred")
         nc.tensor.transpose(out=columns_ps[:], in_=vector_rows[:], identity=ident[:])
@@ -103,7 +103,6 @@ def tile_vocohead_pa_kernel(tc, z1, g1, be1, W2, b2, out):
 
         banks = {}
         sumsq = {}
-        spread = {}
         inverse = {}
         gain = {}
         planes = {}
@@ -111,13 +110,12 @@ def tile_vocohead_pa_kernel(tc, z1, g1, be1, W2, b2, out):
         w_grouped = {}
 
         def centre(pair, j):
-            b, first = pair // 2, (pair % 2) * PAIR_CHUNKS + j * PACK
             bank = centred_pool.tile([P, PACK, P], F32, tag="centred")
             for t in range(PACK):
-                a = first + t
+                i = j * PACK + t
                 nc.tensor.matmul(
                     out=bank[:, t, :],
-                    lhsT=z_sb[b][:, a * P : (a + 1) * P],
+                    lhsT=z_sb[pair][:, i * P : (i + 1) * P],
                     rhs=centre_matrix[:],
                     start=True,
                     stop=True,
@@ -135,19 +133,15 @@ def tile_vocohead_pa_kernel(tc, z1, g1, be1, W2, b2, out):
                     accum_out=sumsq[pair][:, i : i + 1],
                 )
 
-        def root(pair):
-            spread[pair] = stats.tile([P, PAIR_CHUNKS], F32, name="spread")
+        def inverse_root(pair):
+            inverse[pair] = stats.tile([P, PAIR_CHUNKS], F32, name="inverse")
             nc.scalar.activation(
-                out=spread[pair][:],
+                out=inverse[pair][:],
                 in_=sumsq[pair][:],
-                func=ACT.Sqrt,
+                func=ACT.Abs_reciprocal_sqrt,
                 bias=one[:, 0:1],
                 scale=1.0 / (P * BN_EPS),
             )
-
-        def invert(pair):
-            inverse[pair] = stats.tile([P, PAIR_CHUNKS], F32, name="inverse")
-            nc.vector.reciprocal(out=inverse[pair][:], in_=spread[pair][:])
 
         def scale_gain(pair):
             first = (pair % 2) * PAIR_CHUNKS
@@ -196,9 +190,8 @@ def tile_vocohead_pa_kernel(tc, z1, g1, be1, W2, b2, out):
                 in_=w_grouped[k][:].rearrange("p n t -> p (n t)"),
             )
 
-        def multiply(b, nb):
-            acc = acc_pool.tile([P, N_TILE], F32, name="acc")
-            for c in range(K_PASSES):
+        def multiply(acc, b, nb, passes):
+            for c in passes:
                 rows = slice((c % 2) * P, (c % 2 + 1) * P)
                 nc.tensor.matmul_mx(
                     out=acc[:],
@@ -209,7 +202,6 @@ def tile_vocohead_pa_kernel(tc, z1, g1, be1, W2, b2, out):
                     start=(c == 0),
                     stop=(c == K_PASSES - 1),
                 )
-            return acc
 
         def add_bias_and_store(acc, b, nb):
             cols = slice(nb * N_TILE, (nb + 1) * N_TILE)
@@ -225,8 +217,7 @@ def tile_vocohead_pa_kernel(tc, z1, g1, be1, W2, b2, out):
         for k in range(W_AHEAD):
             quantise_w(k)
         squares(0)
-        root(0)
-        invert(0)
+        inverse_root(0)
         scale_gain(0)
 
         b2_all = const.tile([P, HO], BF16)
@@ -248,6 +239,7 @@ def tile_vocohead_pa_kernel(tc, z1, g1, be1, W2, b2, out):
 
         multiplied = set()
         in_psum = []
+        last_tiles = []
         slot = 0
         while len(multiplied) < GROUPS * N_BLOCKS or in_psum:
             if slot + 1 < PAIRS:
@@ -258,15 +250,13 @@ def tile_vocohead_pa_kernel(tc, z1, g1, be1, W2, b2, out):
                 if slot + 2 < PAIRS:
                     centre(slot + 2, j)
                 if j == 0 and slot + 1 < PAIRS:
-                    root(slot + 1)
+                    inverse_root(slot + 1)
 
             k = slot + W_AHEAD
             if slot + 1 < PAIRS:
-                invert(slot + 1)
+                scale_gain(slot + 1)
             if 1 <= slot <= PAIRS:
                 interleave_h(slot - 1)
-            if slot + 1 < PAIRS:
-                scale_gain(slot + 1)
             if k < W_OPERANDS:
                 interleave_w(k)
             if 1 <= slot <= PAIRS:
@@ -277,11 +267,23 @@ def tile_vocohead_pa_kernel(tc, z1, g1, be1, W2, b2, out):
             if k < W_OPERANDS:
                 quantise_w(k)
 
-            groups_ready = min(slot // 2, GROUPS)
+            groups_ready = min(slot // 2, GROUPS - 1)
             blocks_ready = min(k + 1, W_OPERANDS) // K_PASSES
             for b in range(groups_ready):
                 for nb in range(blocks_ready):
                     if (b, nb) not in multiplied and len(in_psum) < ACC_BANKS:
                         multiplied.add((b, nb))
-                        in_psum.append((multiply(b, nb), b, nb))
+                        acc = acc_pool.tile([P, N_TILE], F32, name="acc")
+                        multiply(acc, b, nb, range(K_PASSES))
+                        in_psum.append((acc, b, nb))
+            if slot == PAIRS - 1:
+                for nb in range(N_BLOCKS):
+                    acc = acc_pool.tile([P, N_TILE], F32, name="acc")
+                    multiply(acc, GROUPS - 1, nb, range(K_PASSES // 2))
+                    last_tiles.append(acc)
+            if slot == PAIRS:
+                for nb in range(N_BLOCKS):
+                    multiplied.add((GROUPS - 1, nb))
+                    multiply(last_tiles[nb], GROUPS - 1, nb, range(K_PASSES // 2, K_PASSES))
+                    in_psum.append((last_tiles[nb], GROUPS - 1, nb))
             slot += 1

@@ -71,12 +71,12 @@ def tile_vocohead_pa_kernel(tc, z1, g1, be1, W2, b2, out):
             )
             w_raw.append(w_tile)
 
-        for pair in range(PAIRS):
-            half = slice((pair % 2) * (H // 2), (pair % 2 + 1) * (H // 2))
-            z_tile = inputs.tile([P, H // 2], BF16, name="z%d" % pair)
-            nc.sync.dma_start(out=z_tile[:], in_=z1[pair // 2, :, half])
+        for b in range(GROUPS):
+            load_weights(2 * b)
+            z_tile = inputs.tile([P, H], BF16, name="z%d" % b)
+            nc.sync.dma_start(out=z_tile[:], in_=z1[b])
             z_sb.append(z_tile)
-            load_weights(pair)
+            load_weights(2 * b + 1)
 
         ident = const.tile([P, P], BF16)
         make_identity(nc, ident[:])
@@ -85,7 +85,7 @@ def tile_vocohead_pa_kernel(tc, z1, g1, be1, W2, b2, out):
         one = const.tile([P, 1], F32)
         nc.vector.memset(one[:], 1.0)
         warm = const.tile([P, 1], F32)
-        nc.scalar.activation(out=warm[:], in_=one[:], func=ACT.Abs_reciprocal_sqrt)
+        nc.scalar.activation(out=warm[:], in_=one[:], func=ACT.Sqrt)
 
         columns_ps = centred_pool.tile([P, P], BF16, tag="centred")
         nc.tensor.transpose(out=columns_ps[:], in_=vector_rows[:], identity=ident[:])
@@ -103,6 +103,7 @@ def tile_vocohead_pa_kernel(tc, z1, g1, be1, W2, b2, out):
 
         banks = {}
         sumsq = {}
+        spread = {}
         inverse = {}
         gain = {}
         planes = {}
@@ -110,12 +111,13 @@ def tile_vocohead_pa_kernel(tc, z1, g1, be1, W2, b2, out):
         w_grouped = {}
 
         def centre(pair, j):
+            b, first = pair // 2, (pair % 2) * PAIR_CHUNKS + j * PACK
             bank = centred_pool.tile([P, PACK, P], F32, tag="centred")
             for t in range(PACK):
-                i = j * PACK + t
+                a = first + t
                 nc.tensor.matmul(
                     out=bank[:, t, :],
-                    lhsT=z_sb[pair][:, i * P : (i + 1) * P],
+                    lhsT=z_sb[b][:, a * P : (a + 1) * P],
                     rhs=centre_matrix[:],
                     start=True,
                     stop=True,
@@ -133,15 +135,19 @@ def tile_vocohead_pa_kernel(tc, z1, g1, be1, W2, b2, out):
                     accum_out=sumsq[pair][:, i : i + 1],
                 )
 
-        def inverse_root(pair):
-            inverse[pair] = stats.tile([P, PAIR_CHUNKS], F32, name="inverse")
+        def root(pair):
+            spread[pair] = stats.tile([P, PAIR_CHUNKS], F32, name="spread")
             nc.scalar.activation(
-                out=inverse[pair][:],
+                out=spread[pair][:],
                 in_=sumsq[pair][:],
-                func=ACT.Abs_reciprocal_sqrt,
+                func=ACT.Sqrt,
                 bias=one[:, 0:1],
                 scale=1.0 / (P * BN_EPS),
             )
+
+        def invert(pair):
+            inverse[pair] = stats.tile([P, PAIR_CHUNKS], F32, name="inverse")
+            nc.vector.reciprocal(out=inverse[pair][:], in_=spread[pair][:])
 
         def scale_gain(pair):
             first = (pair % 2) * PAIR_CHUNKS
@@ -170,7 +176,14 @@ def tile_vocohead_pa_kernel(tc, z1, g1, be1, W2, b2, out):
                 out=h_grouped[pair][:, 0, :, :].rearrange("p (m i) t -> p m t i", i=4),
                 in_=planes[pair][:, :, 0, :].rearrange("p t (m i) -> p m t i", i=4),
             )
-            interleave(nc, h_grouped[pair][:, 1, :, :], planes[pair][:, :, 1, :])
+            nc.gpsimd.tensor_scalar(
+                out=h_grouped[pair][:, 1, :, :].rearrange("p (m i) t -> p m t i", i=4),
+                in0=planes[pair][:, :, 1, :].rearrange("p t (m i) -> p m t i", i=4),
+                scalar1=1.0,
+                scalar2=0.0,
+                op0=ALU.mult,
+                op1=ALU.add,
+            )
 
         def quantise_h(pair):
             nc.vector.quantize_mx(
@@ -190,8 +203,9 @@ def tile_vocohead_pa_kernel(tc, z1, g1, be1, W2, b2, out):
                 in_=w_grouped[k][:].rearrange("p n t -> p (n t)"),
             )
 
-        def multiply(acc, b, nb, passes):
-            for c in passes:
+        def multiply(b, nb):
+            acc = acc_pool.tile([P, N_TILE], F32, name="acc")
+            for c in range(K_PASSES):
                 rows = slice((c % 2) * P, (c % 2 + 1) * P)
                 nc.tensor.matmul_mx(
                     out=acc[:],
@@ -202,6 +216,7 @@ def tile_vocohead_pa_kernel(tc, z1, g1, be1, W2, b2, out):
                     start=(c == 0),
                     stop=(c == K_PASSES - 1),
                 )
+            return acc
 
         def add_bias_and_store(acc, b, nb):
             cols = slice(nb * N_TILE, (nb + 1) * N_TILE)
@@ -217,7 +232,8 @@ def tile_vocohead_pa_kernel(tc, z1, g1, be1, W2, b2, out):
         for k in range(W_AHEAD):
             quantise_w(k)
         squares(0)
-        inverse_root(0)
+        root(0)
+        invert(0)
         scale_gain(0)
 
         b2_all = const.tile([P, HO], BF16)
@@ -239,7 +255,6 @@ def tile_vocohead_pa_kernel(tc, z1, g1, be1, W2, b2, out):
 
         multiplied = set()
         in_psum = []
-        last_tiles = []
         slot = 0
         while len(multiplied) < GROUPS * N_BLOCKS or in_psum:
             if slot + 1 < PAIRS:
@@ -250,13 +265,15 @@ def tile_vocohead_pa_kernel(tc, z1, g1, be1, W2, b2, out):
                 if slot + 2 < PAIRS:
                     centre(slot + 2, j)
                 if j == 0 and slot + 1 < PAIRS:
-                    inverse_root(slot + 1)
+                    root(slot + 1)
 
             k = slot + W_AHEAD
             if slot + 1 < PAIRS:
-                scale_gain(slot + 1)
+                invert(slot + 1)
             if 1 <= slot <= PAIRS:
                 interleave_h(slot - 1)
+            if slot + 1 < PAIRS:
+                scale_gain(slot + 1)
             if k < W_OPERANDS:
                 interleave_w(k)
             if 1 <= slot <= PAIRS:
@@ -267,23 +284,11 @@ def tile_vocohead_pa_kernel(tc, z1, g1, be1, W2, b2, out):
             if k < W_OPERANDS:
                 quantise_w(k)
 
-            groups_ready = min(slot // 2, GROUPS - 1)
+            groups_ready = min(slot // 2, GROUPS)
             blocks_ready = min(k + 1, W_OPERANDS) // K_PASSES
             for b in range(groups_ready):
                 for nb in range(blocks_ready):
                     if (b, nb) not in multiplied and len(in_psum) < ACC_BANKS:
                         multiplied.add((b, nb))
-                        acc = acc_pool.tile([P, N_TILE], F32, name="acc")
-                        multiply(acc, b, nb, range(K_PASSES))
-                        in_psum.append((acc, b, nb))
-            if slot == PAIRS - 1:
-                for nb in range(N_BLOCKS):
-                    acc = acc_pool.tile([P, N_TILE], F32, name="acc")
-                    multiply(acc, GROUPS - 1, nb, range(K_PASSES // 2))
-                    last_tiles.append(acc)
-            if slot == PAIRS:
-                for nb in range(N_BLOCKS):
-                    multiplied.add((GROUPS - 1, nb))
-                    multiply(last_tiles[nb], GROUPS - 1, nb, range(K_PASSES // 2, K_PASSES))
-                    in_psum.append((last_tiles[nb], GROUPS - 1, nb))
+                        in_psum.append((multiply(b, nb), b, nb))
             slot += 1

from contextlib import ExitStack

import concourse.mybir as mybir
from concourse.masks import make_identity

FP8X4 = mybir.dt.float8_e4m3fn_x4
BF16 = mybir.dt.bfloat16
F32 = mybir.dt.float32
U32 = mybir.dt.uint32
U8 = mybir.dt.uint8
ACT = mybir.ActivationFunctionType
ALU = mybir.AluOpType

P = 128
PACK = 4
GROUPS = 8
H = 2048
HO = 2048
K_PASSES = H // (P * PACK)
CHUNKS = H // P
N_TILE = 512
N_BLOCKS = HO // N_TILE
BN_EPS = 1e-5

PAIRS = 2 * GROUPS
PAIR_CHUNKS = 2 * PACK
W_OPERANDS = N_BLOCKS * K_PASSES
W_AHEAD = 2
ACC_BANKS = 4

FLOPS = 2 * GROUPS * P * H * HO


def interleave(nc, grouped, planes):
    nc.vector.tensor_copy(
        out=grouped.rearrange("p (m i) t -> p m t i", i=4),
        in_=planes.rearrange("p t (m i) -> p m t i", i=4),
    )


def tile_vocohead_pa_kernel(tc, z1, g1, be1, W2, b2, out):
    nc = tc.nc
    with ExitStack() as ctx:
        const = ctx.enter_context(tc.tile_pool(name="const", bufs=1))
        inputs = ctx.enter_context(tc.tile_pool(name="inputs", bufs=1))
        keep = ctx.enter_context(tc.tile_pool(name="keep", bufs=1))
        stage = ctx.enter_context(tc.tile_pool(name="stage", bufs=3))
        stats = ctx.enter_context(tc.tile_pool(name="stats", bufs=4))
        results = ctx.enter_context(tc.tile_pool(name="results", bufs=6))
        centred_pool = ctx.enter_context(tc.psum_pool(name="centred", bufs=4))
        acc_pool = ctx.enter_context(tc.psum_pool(name="acc", bufs=ACC_BANKS))

        vector_rows = const.tile([P, P], BF16)
        nc.vector.memset(vector_rows[64:128, :], 0.0)
        for i, vector in enumerate((g1, be1, b2, b2)):
            nc.scalar.dma_start(
                out=vector_rows[i * CHUNKS : (i + 1) * CHUNKS, :],
                in_=vector.rearrange("(a p) -> a p", p=P),
            )
        z_sb = []
        w_raw = []

        def load_weights(k):
            nb, c = divmod(k, K_PASSES)
            w_tile = inputs.tile([P, PACK, N_TILE], BF16, name="w%d" % k)
            nc.sync.dma_start(
                out=w_tile[:],
                in_=W2[
                    c * PACK * P : (c + 1) * PACK * P, nb * N_TILE : (nb + 1) * N_TILE
                ].rearrange("(t p) n -> p t n", p=P),
            )
            w_raw.append(w_tile)

        for b in range(GROUPS):
            load_weights(2 * b)
            z_tile = inputs.tile([P, H], BF16, name="z%d" % b)
            nc.sync.dma_start(out=z_tile[:], in_=z1[b])
            z_sb.append(z_tile)
            load_weights(2 * b + 1)

        ident = const.tile([P, P], BF16)
        make_identity(nc, ident[:])
        centre_matrix = const.tile([P, P], BF16)
        nc.vector.tensor_scalar_add(out=centre_matrix[:], in0=ident[:], scalar1=-1.0 / P)
        one = const.tile([P, 1], F32)
        nc.vector.memset(one[:], 1.0)
        warm = const.tile([P, 1], F32)
        nc.scalar.activation(out=warm[:], in_=one[:], func=ACT.Sqrt)

        columns_ps = centred_pool.tile([P, P], BF16, tag="centred")
        nc.tensor.transpose(out=columns_ps[:], in_=vector_rows[:], identity=ident[:])
        gain0 = const.tile([P, CHUNKS], F32)
        nc.vector.tensor_scalar_mul(out=gain0[:], in0=columns_ps[:, 0:CHUNKS], scalar1=BN_EPS**-0.5)
        shift = const.tile([P, CHUNKS], F32)
        nc.vector.tensor_copy(out=shift[:], in_=columns_ps[:, CHUNKS : 2 * CHUNKS])
        b2_columns = const.tile([P, CHUNKS], BF16)
        nc.vector.tensor_copy(out=b2_columns[:], in_=columns_ps[:, 2 * CHUNKS : 3 * CHUNKS])

        w_codes = keep.tile([P, W_OPERANDS, N_TILE], U32, align_bytes=64)
        w_scales = keep.tile([P, W_OPERANDS, N_TILE], U8, align_bytes=64)
        h_codes = keep.tile([P, PAIRS, 2 * P], U32, align_bytes=64)
        h_scales = keep.tile([P, PAIRS, 2 * P], U8, align_bytes=64)

        banks = {}
        sumsq = {}
        spread = {}
        inverse = {}
        gain = {}
        planes = {}
        h_grouped = {}
        w_grouped = {}

        def centre(pair, j):
            b, first = pair // 2, (pair % 2) * PAIR_CHUNKS + j * PACK
            bank = centred_pool.tile([P, PACK, P], F32, tag="centred")
            for t in range(PACK):
                a = first + t
                nc.tensor.matmul(
                    out=bank[:, t, :],
                    lhsT=z_sb[b][:, a * P : (a + 1) * P],
                    rhs=centre_matrix[:],
                    start=True,
                    stop=True,
                )
            banks[(pair, j)] = bank

        def squares(pair):
            sumsq[pair] = stats.tile([P, PAIR_CHUNKS], F32, name="sumsq")
            unread = stage.tile([P, PAIR_CHUNKS, P], BF16, name="unread")
            for i in range(PAIR_CHUNKS):
                nc.scalar.activation(
                    out=unread[:, i, :],
                    in_=banks[(pair, i // PACK)][:, i % PACK, :],
                    func=ACT.Square,
                    accum_out=sumsq[pair][:, i : i + 1],
                )

        def root(pair):
            spread[pair] = stats.tile([P, PAIR_CHUNKS], F32, name="spread")
            nc.scalar.activation(
                out=spread[pair][:],
                in_=sumsq[pair][:],
                func=ACT.Sqrt,
                bias=one[:, 0:1],
                scale=1.0 / (P * BN_EPS),
            )

        def invert(pair):
            inverse[pair] = stats.tile([P, PAIR_CHUNKS], F32, name="inverse")
            nc.vector.reciprocal(out=inverse[pair][:], in_=spread[pair][:])

        def scale_gain(pair):
            first = (pair % 2) * PAIR_CHUNKS
            gain[pair] = stats.tile([P, PAIR_CHUNKS], F32, name="gain")
            nc.vector.tensor_mul(
                out=gain[pair][:], in0=inverse[pair][:], in1=gain0[:, first : first + PAIR_CHUNKS]
            )

        def normalise(pair, j):
            if j == 0:
                planes[pair] = stage.tile([P, PACK, 2, P], BF16, name="planes")
            for t in range(PACK):
                i = j * PACK + t
                a = (pair % 2) * PAIR_CHUNKS + i
                nc.scalar.activation(
                    out=planes[pair][:, t, j, :],
                    in_=banks[(pair, j)][:, t, :],
                    func=ACT.Relu,
                    bias=shift[:, a : a + 1],
                    scale=gain[pair][:, i : i + 1],
                )

        def interleave_h(pair):
            h_grouped[pair] = stage.tile([P, 2, P, PACK], BF16, align_bytes=64, name="h_grouped")
            nc.scalar.copy(
                out=h_grouped[pair][:, 0, :, :].rearrange("p (m i) t -> p m t i", i=4),
                in_=planes[pair][:, :, 0, :].rearrange("p t (m i) -> p m t i", i=4),
            )
            nc.gpsimd.tensor_scalar(
                out=h_grouped[pair][:, 1, :, :].rearrange("p (m i) t -> p m t i", i=4),
                in0=planes[pair][:, :, 1, :].rearrange("p t (m i) -> p m t i", i=4),
                scalar1=1.0,
                scalar2=0.0,
                op0=ALU.mult,
                op1=ALU.add,
            )

        def quantise_h(pair):
            nc.vector.quantize_mx(
                out=h_codes[:, pair, :].bitcast(FP8X4),
                scales=h_scales[:, pair, :],
                in_=h_grouped[pair][:].rearrange("p j r t -> p (j r t)"),
            )

        def interleave_w(k):
            w_grouped[k] = stage.tile([P, N_TILE, PACK], BF16, align_bytes=64, name="w_grouped")
            interleave(nc, w_grouped[k][:], w_raw[k][:])

        def quantise_w(k):
            nc.vector.quantize_mx(
                out=w_codes[:, k, :].bitcast(FP8X4),
                scales=w_scales[:, k, :],
                in_=w_grouped[k][:].rearrange("p n t -> p (n t)"),
            )

        def multiply(b, nb):
            acc = acc_pool.tile([P, N_TILE], F32, name="acc")
            for c in range(K_PASSES):
                rows = slice((c % 2) * P, (c % 2 + 1) * P)
                nc.tensor.matmul_mx(
                    out=acc[:],
                    lhsT=h_codes[:, 2 * b + c // 2, rows].bitcast(FP8X4),
                    lhsT_scale=h_scales[:, 2 * b + c // 2, rows],
                    rhs=w_codes[:, K_PASSES * nb + c, :].bitcast(FP8X4),
                    rhs_scale=w_scales[:, K_PASSES * nb + c, :],
                    start=(c == 0),
                    stop=(c == K_PASSES - 1),
                )
            return acc

        def add_bias_and_store(acc, b, nb):
            cols = slice(nb * N_TILE, (nb + 1) * N_TILE)
            result = results.tile([P, N_TILE], F32, name="result")
            nc.vector.tensor_tensor(out=result[:], in0=acc[:], in1=b2_all[:, cols], op=ALU.add)
            nc.sync.dma_start(out=out[b, :, cols], in_=result[:])

        for pair in (0, 1):
            centre(pair, 0)
            centre(pair, 1)
        for k in range(W_AHEAD):
            interleave_w(k)
        for k in range(W_AHEAD):
            quantise_w(k)
        squares(0)
        root(0)
        invert(0)
        scale_gain(0)

        b2_all = const.tile([P, HO], BF16)
        for nb in range(N_BLOCKS):
            b2_ps = acc_pool.tile([P, PACK, P], F32, name="acc")
            for t in range(PACK):
                a = PACK * nb + t
                nc.tensor.matmul(
                    out=b2_ps[:, t, :],
                    lhsT=b2_columns[:, a : a + 1].to_broadcast([P, P]),
                    rhs=ident[:],
                    start=True,
                    stop=True,
                )
            nc.vector.tensor_copy(
                out=b2_all[:, nb * N_TILE : (nb + 1) * N_TILE],
                in_=b2_ps[:].rearrange("p t n -> p (t n)"),
            )

        multiplied = set()
        in_psum = []
        slot = 0
        while len(multiplied) < GROUPS * N_BLOCKS or in_psum:
            if slot + 1 < PAIRS:
                squares(slot + 1)
            for j in range(2):
                if slot < PAIRS:
                    normalise(slot, j)
                if slot + 2 < PAIRS:
                    centre(slot + 2, j)
                if j == 0 and slot + 1 < PAIRS:
                    root(slot + 1)

            k = slot + W_AHEAD
            if slot + 1 < PAIRS:
                invert(slot + 1)
            if 1 <= slot <= PAIRS:
                interleave_h(slot - 1)
            if slot + 1 < PAIRS:
                scale_gain(slot + 1)
            if k < W_OPERANDS:
                interleave_w(k)
            if 1 <= slot <= PAIRS:
                quantise_h(slot - 1)
            for acc, b, nb in in_psum:
                add_bias_and_store(acc, b, nb)
            in_psum = []
            if k < W_OPERANDS:
                quantise_w(k)

            groups_ready = min(slot // 2, GROUPS)
            blocks_ready = min(k + 1, W_OPERANDS) // K_PASSES
            for b in range(groups_ready):
                for nb in range(blocks_ready):
                    if (b, nb) not in multiplied and len(in_psum) < ACC_BANKS:
                        multiplied.add((b, nb))
                        in_psum.append((multiply(b, nb), b, nb))
            slot += 1
